import numpy as np
import ml_dtypes


def mxq(x, axis, fmt="e4m3"):
    dtype, down = {"e4m3": (ml_dtypes.float8_e4m3fn, 7), "e5m2": (ml_dtypes.float8_e5m2, 14)}[fmt]
    v = np.moveaxis(np.asarray(x, np.float32).astype(ml_dtypes.bfloat16).astype(np.float64), axis, -1)
    blocks = v.reshape(v.shape[:-1] + (-1, 32))
    amax = np.abs(blocks).max(-1, keepdims=True)
    byte = np.maximum(np.where(amax > 0, np.frexp(amax)[1] - 1 + 127, 0) - down, 1)
    scale = np.exp2(byte - 127.0)
    codes = (blocks / scale).astype(np.float32).astype(dtype).astype(np.float64)
    return np.moveaxis((codes * scale).reshape(v.shape), -1, axis)


WIDE = False


def mx_kscale(k):
    if not WIDE:
        return np.ones(k)
    levels = np.array([18, -18])
    if k % 512:
        return np.exp2(np.random.permutation(np.resize(levels, k // 32))).repeat(32)
    a = np.empty((k // 512, 16))
    for p in range(k // 512):
        a[p, :8] = np.random.permutation(np.resize(levels, 8))
        for g in range(8):
            far = levels[np.abs(levels - a[p, g]) >= 10]
            a[p, g + 8] = far[np.random.randint(len(far))]
    return np.exp2(a.ravel()).repeat(32)


BF16 = ml_dtypes.bfloat16


def bf(x):
    return np.asarray(x, np.float32).astype(BF16)


def f64(x):
    return np.asarray(x).astype(np.float64)


B, S, DIM, HDIM = 2, 512, 512, 2048
T = B * S


def setup_inputs():
    s = mx_kscale(T).reshape(B, S, 1)
    u = mx_kscale(DIM)
    v = mx_kscale(HDIM)
    x0 = bf(np.random.standard_normal((B, S, DIM)))
    W1_0 = bf(np.random.standard_normal((HDIM, DIM)) * (1.0 / np.sqrt(DIM)))
    W2_0 = bf(np.random.standard_normal((HDIM, DIM)) * (1.0 / np.sqrt(HDIM)))
    g = bf(2.0 * np.random.standard_normal((B, S, DIM)) * np.exp2(np.random.randint(-6, 1, (B, S, 1))) / s * u)
    pre = f64(x0) @ f64(W1_0).T
    return {"x": bf(f64(x0) * s),
            "W1": bf(f64(W1_0) / v[:, None]),
            "W2": bf(f64(W2_0) * v[:, None] / u[None, :]),
            "pre": np.asarray(pre, np.float32),
            "grad_out": g}


def reference(x, W1, W2, pre, grad_out):
    xf = f64(x).reshape(T, DIM)
    g = f64(grad_out).reshape(T, DIM)
    zf = f64(pre).reshape(T, HDIM)
    dh = mxq(g, 1, "e5m2") @ mxq(f64(W2), 1, "e4m3").T
    dz1 = dh * (2.0 * np.maximum(zf, 0.0))
    dx = mxq(dz1, 1, "e5m2") @ mxq(f64(W1), 0, "e4m3")
    dW1 = mxq(dz1, 0, "e5m2").T @ mxq(xf, 0, "e4m3")
    return dx.reshape(B, S, DIM), dW1

@@ -1,0 +1,392 @@
+from contextlib import ExitStack
+
+import concourse.mybir as mybir
+from concourse.masks import make_identity
+
+B, S, DIM, HDIM = 2, 512, 512, 2048
+P = 128
+CH = 512
+NC = HDIM // CH
+UNITS = [(0, 0), (0, 1), (1, 0), (1, 1), (0, 2), (0, 3), (1, 2), (1, 3)]
+FLOPS = 3 * 2 * B * S * DIM * HDIM
+
+F32 = mybir.dt.float32
+BF16 = mybir.dt.bfloat16
+U32 = mybir.dt.uint32
+U8 = mybir.dt.uint8
+E4 = mybir.dt.float8_e4m3fn_x4
+E5 = mybir.dt.float8_e5m2_x4
+ALU = mybir.AluOpType
+ACTF = mybir.ActivationFunctionType
+
+
+def tile_mlp_v_kernel(tc, x, w1, w2, pre, grad_out, out_0, out_1):
+    nc = tc.nc
+    with ExitStack() as ctx:
+        keep = ctx.enter_context(tc.tile_pool(name="keep", bufs=1))
+        stream = ctx.enter_context(tc.tile_pool(name="stream", bufs=2))
+        psum = ctx.enter_context(tc.psum_pool(name="psum", bufs=2))
+        ctx.enter_context(tc.manual_schedule())
+
+        ident = keep.tile([P, P], F32, name="ident")
+        make_identity(nc, ident[:])
+        warm = keep.tile([P, 1], F32, name="warm")
+        nc.vector.memset(warm[:], 0.0)
+        nc.scalar.activation(out=warm[:], in_=warm[:], func=ACTF.Copy, scale=2.0)
+
+        g_raw, x_raw, w1_raw, w2_raw, pre_t = {}, {}, {}, {}, {}
+
+        def load_g(b):
+            t = keep.tile([P, 4, DIM], BF16, name="g_raw%d" % b)
+            src = grad_out[b].rearrange("(p j) d -> p j d", j=4)
+            for i in range(0, 4, 2):
+                nc.sync.dma_start(out=t[:, i : i + 2, :], in_=src[:, i : i + 2, :])
+            g_raw[b] = t
+
+        def load_x(b):
+            t = keep.tile([P, 4, DIM], BF16, name="x_raw%d" % b)
+            nc.sync.dma_start(out=t[:], in_=x[b].rearrange("(p j) d -> p j d", j=4))
+            x_raw[b] = t
+
+        def load_w1(c):
+            t = stream.tile([P, 4, DIM], BF16, name="w1_raw", bufs=3)
+            nc.sync.dma_start(out=t[:], in_=w1[CH * c : CH * c + CH, :].rearrange("(p j) d -> p j d", j=4))
+            w1_raw[c] = t
+
+        def load_w2(c, parts=1):
+            t = stream.tile([P, 2, 2, DIM], BF16, name="w2_raw", bufs=3)
+            src = w2[CH * c : CH * c + CH, :].rearrange("(s p e) d -> p s e d", s=2, e=2)
+            n = 2 // parts
+            for i in range(parts):
+                nc.sync.dma_start(out=t[:, n * i : n * i + n, :, :], in_=src[:, n * i : n * i + n, :, :])
+            w2_raw[c] = t
+
+        def load_pre(k, halves=1):
+            b, c = UNITS[k]
+            t = stream.tile([P, 4, CH], F32, name="pre_t", bufs=5)
+            src = pre[b].rearrange("(p j) h -> p j h", j=4)
+            n = 4 // halves
+            for i in range(halves):
+                nc.sync.dma_start(
+                    out=t[:, n * i : n * i + n, :], in_=src[:, n * i : n * i + n, CH * c : CH * c + CH]
+                )
+            pre_t[k] = t
+
+        def quantise(store, i, name, grouped, dt, lo=0, hi=CH):
+            if lo == 0:
+                codes = keep.tile([P, CH], U32, name=name + "_codes%s" % str(i), align_bytes=64)
+                scales = keep.tile([P, CH], U8, name=name + "_scales%s" % str(i), align_bytes=64)
+                store[i] = (codes, scales)
+            codes, scales = store[i]
+            nc.vector.quantize_mx(
+                out=codes[:, lo:hi].bitcast(dt), scales=scales[:, lo:hi], in_=grouped[:, 4 * lo : 4 * hi]
+            )
+
+        gq, w2q, w1q, xq, hq, tq = {}, {}, {}, {}, {}, {}
+        g_gr, w2_gr, w1_gr, x_gr = {}, {}, {}, {}
+
+        def bank_of_transposes(words):
+            xt = psum.tile([P, 4, P], F32, name="xt", bufs=2)
+            for i in range(4):
+                nc.tensor.transpose(xt[:, i, :], words[i], ident[:])
+            return xt
+
+        def copy_words(eng, out, in_):
+            if eng == "s":
+                nc.scalar.copy(out=out, in_=in_)
+            else:
+                nc.vector.tensor_copy(out=out, in_=in_)
+
+        def prep_g(b, half, eng="s"):
+            if half == 0:
+                g_gr[b] = stream.tile([P, 4 * CH], BF16, name="grouped_in", bufs=3, align_bytes=64)
+            words = g_raw[b][:].bitcast(F32)
+            xt = bank_of_transposes([words[:, 2 * half + i // 2, i % 2 : 256 : 2] for i in range(4)])
+            copy_words(
+                eng,
+                out=g_gr[b][:].bitcast(F32)[:, CH * half : CH * half + CH].rearrange("k (j n u) -> k j n u", j=2, u=2),
+                in_=xt[:].rearrange("k (j u) n -> k j n u", u=2),
+            )
+
+        def quant_g(b, half):
+            quantise(gq, b, "gq", g_gr[b], E5, 256 * half, 256 * half + 256)
+
+        def prep_w2(c, s, eng="s"):
+            if s == 0:
+                w2_gr[c] = stream.tile([P, 4 * CH], BF16, name="grouped_in", bufs=3, align_bytes=64)
+            words = w2_raw[c][:].rearrange("p s e d -> p (s e d)").bitcast(F32)
+            xt = bank_of_transposes(
+                [words[:, 256 * (2 * s + i // 2) + i % 2 : 256 * (2 * s + i // 2) + 256 : 2] for i in range(4)]
+            )
+            copy_words(
+                eng,
+                out=w2_gr[c][:].bitcast(F32)[:, CH * s : CH * s + CH].rearrange("k (n i) -> k n i", i=4),
+                in_=xt[:].rearrange("k i n -> k n i"),
+            )
+
+        def quant_w2(c, s=None):
+            if s is None:
+                quantise(w2q, c, "w2q", w2_gr[c], E4)
+            else:
+                quantise(w2q, c, "w2q", w2_gr[c], E4, 256 * s, 256 * s + 256)
+
+        def interleave(eng, dst, src, lo, hi):
+            o = dst[:, 4 * lo : 4 * hi].rearrange("p (c i t) -> p c t i", i=4, t=4)
+            i = src[:, :, lo:hi].rearrange("p t (c i) -> p c t i", i=4)
+            if eng == "s":
+                nc.scalar.copy(out=o, in_=i)
+            elif eng == "v":
+                nc.vector.tensor_copy(out=o, in_=i)
+            else:
+                nc.gpsimd.tensor_scalar(out=o, in0=i, scalar1=1.0, scalar2=0.0, op0=ALU.mult, op1=ALU.add)
+
+        def inter_raw(store, raw, i, eng, lo=0, hi=512):
+            if lo == 0:
+                store[i] = stream.tile([P, 4 * CH], BF16, name="grouped_raw", bufs=3, align_bytes=64)
+            interleave(eng, store[i], raw[i], lo, hi)
+
+        d_t, i_t, g_t = {}, {}, {}
+        dh_t = {}
+
+        def dh(k, j):
+            b, c = UNITS[k]
+            t = psum.tile([P, CH], F32, name="dh", bufs=3)
+            nc.tensor.matmul_mx(
+                out=t[:],
+                lhsT=gq[b][0][:, P * j : P * j + P].bitcast(E5),
+                lhsT_scale=gq[b][1][:, P * j : P * j + P],
+                rhs=w2q[c][0][:].bitcast(E4),
+                rhs_scale=w2q[c][1][:],
+                start=True,
+                stop=True,
+            )
+            dh_t[k, j] = t
+
+        def dz(k, j):
+            if j == 0:
+                d_t[k] = stream.tile([P, 4, CH], BF16, name="dz", bufs=3, align_bytes=64)
+            nc.vector.scalar_tensor_tensor(
+                out=d_t[k][:, j, :], in0=pre_t[k][:, j, :], scalar=0.0, in1=dh_t[k, j][:], op0=ALU.max, op1=ALU.mult
+            )
+
+        def flip(k, j0, n=2, eng="s"):
+            if j0 == 0:
+                g_t[k] = stream.tile([P, 4 * CH], BF16, name="dz_h", bufs=3, align_bytes=64)
+            words = d_t[k][:].bitcast(F32)
+            xt = psum.tile([P, 4, P], F32, name="xt", bufs=2)
+            for i in range(2 * n):
+                nc.tensor.transpose(xt[:, i, :], words[:, j0 + i // 2, i % 2 : 256 : 2], ident[:])
+            copy_words(
+                eng,
+                out=g_t[k][:].bitcast(F32)[:, 256 * j0 : 256 * (j0 + n)].rearrange("k (j n u) -> k j n u", j=n, u=2),
+                in_=xt[:, 0 : 2 * n, :].rearrange("k (j u) n -> k j n u", u=2),
+            )
+
+        def quant_h(k, j0=0, n=4):
+            quantise(hq, UNITS[k], "hq", g_t[k], E5, P * j0, P * (j0 + n))
+
+        def quant_t(k, lo=0, hi=CH):
+            quantise(tq, UNITS[k], "tq", i_t[k], E5, lo, hi)
+
+        def inter_dz(k, shares):
+            i_t[k] = stream.tile([P, 4 * CH], BF16, name="dz_t", bufs=3, align_bytes=64)
+            for eng, lo, hi in shares:
+                interleave(eng, i_t[k], d_t[k], lo, hi)
+
+        def bank(tag):
+            if tag == "xt":
+                t = psum.tile([P, 4, P], F32, name="xt", bufs=2)
+                return t[:].rearrange("p a b -> p (a b)")
+            if tag == "dh":
+                t = psum.tile([P, CH], F32, name="dh", bufs=3)
+                return t[:]
+            t = psum.tile([P, DIM], F32, name="acc", bufs=3)
+            return t[:]
+
+        def leave(acc, dst, eng):
+            res = stream.tile([P, DIM], F32, name="res", bufs=8)
+            if eng == "s":
+                nc.scalar.activation(out=res[:], in_=acc, func=ACTF.Copy, scale=2.0)
+            else:
+                nc.vector.tensor_scalar(out=res[:], in0=acc, scalar1=2.0, scalar2=None, op0=ALU.mult)
+            nc.sync.dma_start(out=dst, in_=res[:])
+
+        def dst_of(kind, a, i):
+            if kind == "dx":
+                return out_0[a].rearrange("(p j) d -> p j d", j=4)[:, i, :]
+            return out_1[CH * a + P * i : CH * a + P * i + P, :]
+
+        opened = {}
+
+        def begin(kind, a, i, tag="acc"):
+            acc = bank(tag)
+            n = NC if kind == "dx" else B
+            for q in range(n - 1):
+                one_pass(acc, kind, a, i, q, n)
+            opened[kind, a, i] = acc
+
+        def one_pass(acc, kind, a, i, q, n):
+            if kind == "dx":
+                lhs, rhs = hq[a, q], w1q[q]
+            else:
+                lhs, rhs = tq[q, a], xq[q]
+            nc.tensor.matmul_mx(
+                out=acc,
+                lhsT=lhs[0][:, P * i : P * i + P].bitcast(E5),
+                lhsT_scale=lhs[1][:, P * i : P * i + P],
+                rhs=rhs[0][:].bitcast(E4),
+                rhs_scale=rhs[1][:],
+                start=(q == 0),
+                stop=(q == n - 1),
+            )
+
+        def finish(kind, a, i, eng):
+            acc = opened[kind, a, i]
+            n = NC if kind == "dx" else B
+            one_pass(acc, kind, a, i, n - 1, n)
+            leave(acc, dst_of(kind, a, i), eng)
+
+        def whole(kind, a, i, eng="s", tag="acc"):
+            begin(kind, a, i, tag)
+            finish(kind, a, i, eng)
+
+        load_w2(0, 2)
+        load_g(0)
+        load_pre(0, 2)
+        load_w2(1)
+        load_pre(1, 2)
+        load_g(1)
+        load_pre(2)
+        load_x(0)
+        load_x(1)
+        load_pre(3)
+        load_w2(2)
+        load_w1(0)
+        load_pre(4)
+        load_w2(3)
+        load_w1(1)
+        load_pre(5)
+        load_w1(2)
+        load_w1(3)
+        load_pre(6)
+        load_pre(7)
+        pending = []
+
+        def emit(n, engs="s"):
+            for i in range(min(n, len(pending))):
+                kind, a, b = pending[0]
+                pending.remove(pending[0])
+                whole(kind, a, b, engs[i % len(engs)])
+
+        prep_w2(0, 0, "s")
+        prep_w2(0, 1, "v")
+        prep_g(0, 0, "s")
+        quant_w2(0)
+        prep_g(0, 1, "s")
+        quant_g(0, 0)
+        dh(0, 0)
+        dh(0, 1)
+        quant_g(0, 1)
+        dh(0, 2)
+
+        XENG = "g"
+        SHARE = [("v", 0, 512)]
+        LAST = [("v", 0, 256), ("s", 256, 512)]
+        for k in range(8):
+            nxt, last = k < 7, k == 7
+            dz(k, 0)
+            dh(k, 3)
+            if last:
+                flip(k, 0, 1)
+            emit(1)
+            if k >= 2:
+                inter_dz(k - 1, SHARE)
+            dz(k, 1)
+            if nxt:
+                flip(k, 0)
+            else:
+                flip(k, 1, 1)
+            if k >= 2:
+                quant_h(k - 1)
+            if k == 1:
+                quant_g(1, 0)
+                quant_g(1, 1)
+            if k == 3:
+                quant_w2(2)
+            if k == 4:
+                quant_w2(3)
+            if nxt and k >= 1:
+                dh(k + 1, 0)
+            emit(1)
+            dz(k, 2)
+            if nxt and k >= 1:
+                dh(k + 1, 1)
+            if last:
+                flip(k, 2, 1)
+            emit(1)
+            if k >= 2:
+                quant_t(k - 1)
+                if k == 3:
+                    pending.extend([("dw", 0, m) for m in range(4)])
+                if k == 4:
+                    pending.extend([("dw", 1, m) for m in range(4)])
+                if k == 6:
+                    pending.extend([("dx", 0, m) for m in range(4)])
+                if k == 7:
+                    pending.extend([("dw", 2, m) for m in range(4)])
+            if last:
+                quant_h(7, 0, 2)
+                emit(4)
+                begin("dx", 1, 0, "dh")
+            dz(k, 3)
+            flip(k, 2) if nxt else flip(k, 3, 1)
+            if nxt and k >= 1:
+                dh(k + 1, 2)
+            if k == 0:
+                inter_dz(0, SHARE)
+                prep_w2(1, 0)
+                prep_w2(1, 1)
+                quant_h(0)
+                quant_w2(1)
+                for j in range(3):
+                    dh(1, j)
+                quant_t(0)
+                prep_g(1, 0)
+                prep_g(1, 1)
+            if k == 2:
+                prep_w2(2, 0)
+                prep_w2(2, 1)
+            if k == 3:
+                prep_w2(3, 0)
+                prep_w2(3, 1)
+            if 2 <= k <= 5:
+                inter_raw(w1_gr, w1_raw, k - 2, "s", 0, 256)
+                inter_raw(w1_gr, w1_raw, k - 2, "s", 256, 512)
+            if k == 1:
+                inter_raw(x_gr, x_raw, 0, "v")
+                inter_raw(x_gr, x_raw, 1, XENG)
+            if k == 2:
+                quantise(xq, 0, "xq", x_gr[0], E4)
+                quantise(xq, 1, "xq", x_gr[1], E4)
+            if 3 <= k <= 6:
+                quantise(w1q, k - 3, "w1q", w1_gr[k - 3], E4)
+            emit(1)
+        begin("dx", 1, 1, "dh")
+        begin("dx", 1, 2)
+        begin("dx", 1, 3)
+        inter_dz(7, LAST)
+        finish("dx", 1, 0, "s")
+        finish("dx", 1, 1, "s")
+        quant_h(7, 2, 2)
+        begin("dw", 3, 0, "dh")
+        begin("dw", 3, 1)
+        begin("dw", 3, 2, "xt")
+        begin("dw", 3, 3, "xt")
+        quant_t(7, 0, 256)
+        finish("dx", 1, 2, "v")
+        finish("dx", 1, 3, "s")
+        finish("dw", 3, 0, "v")
+        quant_t(7, 256, 512)
+        finish("dw", 3, 1, "s")
+        finish("dw", 3, 2, "v")
+        finish("dw", 3, 3, "s")

@@ -3,21 +3,90 @@ from contextlib import ExitStack
 import concourse.mybir as mybir
 from concourse.masks import make_identity
 
-B, S, DIM, HDIM = 2, 512, 512, 2048
+BATCH, SEQ, DIM, HIDDEN = 2, 512, 512, 2048
 P = 128
-CH = 512
-NC = HDIM // CH
-UNITS = [(0, 0), (0, 1), (1, 0), (1, 1), (0, 2), (0, 3), (1, 2), (1, 3)]
-FLOPS = 3 * 2 * B * S * DIM * HDIM
+PACK = 4
+PASS = P * PACK
+HALF = HIDDEN // 2
+FLOPS = 3 * 2 * BATCH * SEQ * DIM * HIDDEN
 
 F32 = mybir.dt.float32
 BF16 = mybir.dt.bfloat16
 U32 = mybir.dt.uint32
 U8 = mybir.dt.uint8
-E4 = mybir.dt.float8_e4m3fn_x4
-E5 = mybir.dt.float8_e5m2_x4
-ALU = mybir.AluOpType
-ACTF = mybir.ActivationFunctionType
+E4M3 = mybir.dt.float8_e4m3fn_x4
+E5M2 = mybir.dt.float8_e5m2_x4
+MULT, ADD, MAX = mybir.AluOpType.mult, mybir.AluOpType.add, mybir.AluOpType.max
+COPY = mybir.ActivationFunctionType.Copy
+
+SCHEDULE = (
+    "load_g.01 load_w2.01 load_g.00 load_w2.00 load_x.0 flip_g.01v flip_w2.010s flip_w2.011v flip_g.00s",
+    "  load_g.10 group_x.00v quant_w2.01 quant_g.00 load_g.11 flip_w2.001v group_x.01s load_pre.0001",
+    "  flip_w2.000s quant_g.01 quant_x.0 flip_g.11s dh.0010 load_pre.0011 quant_w2.00 load_x.1 dh.0001",
+    "dz.0010",
+    "dz.0001 group_x.11s dh.0000 flip_g.10s dh.0011 dh.0012 load_w2.12 load_pre.0021 group_x.10g",
+    "dz.0000 flip.000s load_pre.0031",
+    "dz.0011 quant_x.1 load_pre.1022 flip_w2.101s quant_g.11 dh.0002 load_pre.1002 dh.0003 flip_w2.100s",
+    "  flip_w2.111s quant_g.10",
+    "dz.0012 dh.0013",
+    "dz.0002 load_pre.0102",
+    "dz.0003 quant_w2.10 dh.1003 group_t.00002s flip.002s",
+    "dz.0013 group_t.00012g flip_w2.110s dh.1013",
+    "dz.1003 dh.1002 flip.001s",
+    "dz.1013 group_t.00102s dh.1000",
+    "dz.1002 dh.1001 flip.103s dh.1011 quant_t.0002",
+    "dz.1001",
+    "dz.1000 flip.003s group_t.00112g group_t.10012s load_w1.0 load_w1.1 dw_pass.020",
+    "dz.1011 load_pre.0122 dh.1010 quant_w2.11 dh.1012 flip.101s group_t.10002g group_w1.00s dh.0101",
+    "  group_w1.01s",
+    "dz.1012",
+    "dz.1010",
+    "dz.0101 dh.0111 load_pre.1122 dw_pass.000 quant_t.0012 dh.0103 flip.100s quant_t.1002 load_w1.2",
+    "  dw_pass.120 quant_h.00004 dw_pass.021 load_pre.1102 quant_h.00104 dw_out.02s",
+    "dz.0111 dh.0113",
+    "dz.0103 flip.102s dw_pass.001 load_w1.3 dh.0100",
+    "dz.0113 dw_pass.030 group_t.10102g dw_pass.031",
+    "dz.0100 group_w1.11g dh.0102 group_t.10112s",
+    "dz.0102 quant_t.1012 dw_out.00s flip.011s group_w1.10s dh.1113 dh.0110 quant_w1.0",
+    "dz.1113 flip.013s",
+    "dz.0110 group_t.01012g dw_pass.100 dw_pass.010 dw_pass.121 dw_pass.011 dh.1102 group_t.01002g dh.1112",
+    "  dw_pass.101 dh.1103 dw_out.12s",
+    "dz.1112 dw_out.10s flip.010s",
+    "dz.1102",
+    "dz.1103 quant_h.10004 dw_pass.130 dh.0112 dh.1110 quant_h.10104 dw_out.01s dw_out.03s dh.1111",
+    "  quant_w1.1 group_w1.20g",
+    "dz.0112 dw_pass.131",
+    "dz.1110 group_w1.21s flip.113s flip.112s dx_pass.030 dx_pass.031 dx_pass.110",
+    "dz.1111 dx_pass.111 dh.1100",
+    "dz.1100 dw_out.13s flip.012s dh.1101 group_w1.30s",
+    "dz.1101 group_w1.31g quant_w1.2 quant_h.01004 quant_h.01104 quant_h.11022 dw_pass.110 dx_pass.130",
+    "  dx_pass.000 dx_pass.001 quant_w1.3 dw_pass.111 flip.110s quant_h.11122 flip.111s quant_h.11002",
+    "  dx_pass.120 dx_pass.121 dx_pass.100 dx_pass.002 dx_pass.020 dx_pass.032 dw_out.11s dx_pass.122",
+    "  group_t.11012s dx_pass.003 dx_pass.033 dx_out.00v dx_pass.101 dx_pass.123 dx_pass.112 dx_pass.102",
+    "  quant_h.11102 dx_pass.103 dx_out.03s group_t.11002v dx_pass.113 dx_out.12s dx_pass.131 dx_out.10s",
+    "  dx_pass.132 dx_pass.133 quant_t.0102 quant_t.1102 dw_pass.200 dx_out.11s dw_pass.230 group_t.11100g",
+    "  dx_out.13v dw_pass.201 dw_pass.231 dw_pass.220 dw_pass.210 dw_pass.221 dw_out.20v dw_out.23v",
+    "  dx_pass.021 group_t.01112g dw_out.22v dx_pass.022 group_t.11111s dx_pass.023 dx_pass.010",
+    "  group_t.11101s dw_pass.211 dx_pass.011 group_t.01102s dx_pass.012 group_t.11110v quant_t.0112",
+    "  dx_pass.013 dw_pass.310 quant_t.1110 dw_pass.311 dx_out.02s quant_t.1111 dw_pass.330 dw_out.21s",
+    "  dx_out.01s dw_pass.331 dw_pass.320 dw_pass.321 dw_pass.300 dw_out.31v dw_out.33v dw_out.32v",
+    "  dw_pass.301 dw_out.30v",
+)
+
+OTHER_BANKS = {
+    ("dw", 0, 1): ("flipped", 2),
+    ("dw", 1, 1): ("dh", 3),
+    ("dw", 2, 0): ("dh", 3),
+    ("dw", 2, 2): ("dh", 3),
+    ("dw", 2, 3): ("dh", 3),
+    ("dw", 3, 0): ("dh", 3),
+    ("dw", 3, 1): ("flipped", 2),
+    ("dw", 3, 3): ("flipped", 2),
+    ("dx", 0, 0): ("dh", 3),
+    ("dx", 0, 2): ("flipped", 2),
+    ("dx", 1, 0): ("flipped", 2),
+    ("dx", 1, 2): ("dh", 3),
+}
 
 
 def tile_mlp_v_kernel(tc, x, w1, w2, pre, grad_out, out_0, out_1):
@@ -32,361 +101,233 @@ def tile_mlp_v_kernel(tc, x, w1, w2, pre, grad_out, out_0, out_1):
         make_identity(nc, ident[:])
         warm = keep.tile([P, 1], F32, name="warm")
         nc.vector.memset(warm[:], 0.0)
-        nc.scalar.activation(out=warm[:], in_=warm[:], func=ACTF.Copy, scale=2.0)
+        nc.scalar.activation(out=warm[:], in_=warm[:], func=COPY, scale=2.0)
 
-        g_raw, x_raw, w1_raw, w2_raw, pre_t = {}, {}, {}, {}, {}
+        raw = {}
+        pre_rows = {}
+        grouped = {}
+        dz = {}
+        banks = {}
+        codes = {}
 
-        def load_g(b):
-            t = keep.tile([P, 4, DIM], BF16, name="g_raw%d" % b)
+        def load_g(b, half):
+            if ("g", b) not in raw:
+                raw["g", b] = keep.tile([P, 4, DIM], BF16, name="g_raw%d" % b)
+            j = slice(2 * half, 2 * half + 2)
             src = grad_out[b].rearrange("(p j) d -> p j d", j=4)
-            for i in range(0, 4, 2):
-                nc.sync.dma_start(out=t[:, i : i + 2, :], in_=src[:, i : i + 2, :])
-            g_raw[b] = t
+            nc.sync.dma_start(out=raw["g", b][:, j, :], in_=src[:, j, :])
 
         def load_x(b):
-            t = keep.tile([P, 4, DIM], BF16, name="x_raw%d" % b)
-            nc.sync.dma_start(out=t[:], in_=x[b].rearrange("(p j) d -> p j d", j=4))
-            x_raw[b] = t
+            raw["x", b] = stream.tile([P, 4, DIM], BF16, name="xw_raw", bufs=4)
+            nc.sync.dma_start(out=raw["x", b][:], in_=x[b].rearrange("(p j) d -> p j d", j=4))
 
-        def load_w1(c):
-            t = stream.tile([P, 4, DIM], BF16, name="w1_raw", bufs=3)
-            nc.sync.dma_start(out=t[:], in_=w1[CH * c : CH * c + CH, :].rearrange("(p j) d -> p j d", j=4))
-            w1_raw[c] = t
+        def load_w1(q):
+            raw["w1", q] = stream.tile([P, 4, DIM], BF16, name="xw_raw", bufs=4)
+            src = w1[PASS * q : PASS * q + PASS, :].rearrange("(p t) d -> p t d", t=4)
+            nc.sync.dma_start(out=raw["w1", q][:], in_=src)
 
-        def load_w2(c, parts=1):
-            t = stream.tile([P, 2, 2, DIM], BF16, name="w2_raw", bufs=3)
-            src = w2[CH * c : CH * c + CH, :].rearrange("(s p e) d -> p s e d", s=2, e=2)
-            n = 2 // parts
-            for i in range(parts):
-                nc.sync.dma_start(out=t[:, n * i : n * i + n, :, :], in_=src[:, n * i : n * i + n, :, :])
-            w2_raw[c] = t
-
-        def load_pre(k, halves=1):
-            b, c = UNITS[k]
-            t = stream.tile([P, 4, CH], F32, name="pre_t", bufs=5)
-            src = pre[b].rearrange("(p j) h -> p j h", j=4)
-            n = 4 // halves
-            for i in range(halves):
+        def load_w2(c, u):
+            if ("v", c) not in raw:
+                raw["v", c] = stream.tile([P, 2, 2, 2, DIM], BF16, name="w2_raw", bufs=2)
+            rows = w2[HALF * c : HALF * c + HALF, :]
+            if u == 2:
                 nc.sync.dma_start(
-                    out=t[:, n * i : n * i + n, :], in_=src[:, n * i : n * i + n, CH * c : CH * c + CH]
+                    out=raw["v", c][:].rearrange("p s u e d -> p s (u e d)"),
+                    in_=rows.rearrange("(s p f) d -> p s (f d)", s=2, f=4),
                 )
-            pre_t[k] = t
+            else:
+                nc.sync.dma_start(
+                    out=raw["v", c][:].rearrange("p s u e d -> p s u (e d)")[:, :, u, :],
+                    in_=rows.rearrange("(s p u e) d -> p s u (e d)", s=2, u=2, e=2)[:, :, u, :],
+                )
 
-        def quantise(store, i, name, grouped, dt, lo=0, hi=CH):
-            if lo == 0:
-                codes = keep.tile([P, CH], U32, name=name + "_codes%s" % str(i), align_bytes=64)
-                scales = keep.tile([P, CH], U8, name=name + "_scales%s" % str(i), align_bytes=64)
-                store[i] = (codes, scales)
-            codes, scales = store[i]
-            nc.vector.quantize_mx(
-                out=codes[:, lo:hi].bitcast(dt), scales=scales[:, lo:hi], in_=grouped[:, 4 * lo : 4 * hi]
+        def load_pre(b, c, j, n):
+            if (b, c, j // 2) not in pre_rows:
+                pre_rows[b, c, j // 2] = stream.tile([P, 2, HALF], F32, name="pre_rows", bufs=5)
+            src = pre[b].rearrange("(p j) h -> p j h", j=4)
+            nc.sync.dma_start(
+                out=pre_rows[b, c, j // 2][:, j % 2 : j % 2 + n, :],
+                in_=src[:, j : j + n, HALF * c : HALF * c + HALF],
             )
 
-        gq, w2q, w1q, xq, hq, tq = {}, {}, {}, {}, {}, {}
-        g_gr, w2_gr, w1_gr, x_gr = {}, {}, {}, {}
-
-        def bank_of_transposes(words):
-            xt = psum.tile([P, 4, P], F32, name="xt", bufs=2)
-            for i in range(4):
-                nc.tensor.transpose(xt[:, i, :], words[i], ident[:])
-            return xt
-
-        def copy_words(eng, out, in_):
-            if eng == "s":
+        def copy_words(engine, out, in_):
+            if engine == "s":
                 nc.scalar.copy(out=out, in_=in_)
             else:
                 nc.vector.tensor_copy(out=out, in_=in_)
 
-        def prep_g(b, half, eng="s"):
-            if half == 0:
-                g_gr[b] = stream.tile([P, 4 * CH], BF16, name="grouped_in", bufs=3, align_bytes=64)
-            words = g_raw[b][:].bitcast(F32)
-            xt = bank_of_transposes([words[:, 2 * half + i // 2, i % 2 : 256 : 2] for i in range(4)])
+        def interleave(engine, out, in_):
+            out = out.rearrange("p (c i t) -> p c t i", i=4, t=4)
+            if engine == "s":
+                nc.scalar.copy(out=out, in_=in_)
+            elif engine == "v":
+                nc.vector.tensor_copy(out=out, in_=in_)
+            else:
+                nc.gpsimd.tensor_scalar(out=out, in0=in_, scalar1=1.0, scalar2=0.0, op0=MULT, op1=ADD)
+
+        def group_tile(key, name, bufs, passes=1):
+            if key not in grouped:
+                grouped[key] = stream.tile([P, passes * PACK * PASS], BF16, name=name, bufs=bufs, align_bytes=64)
+            return grouped[key]
+
+        def quantise(key, dtype, src, lo, hi, base=0):
+            if key not in codes:
+                label = "_".join([str(k) for k in key])
+                codes[key] = (
+                    keep.tile([P, PASS], U32, name="codes_" + label, align_bytes=64),
+                    keep.tile([P, PASS], U8, name="scales_" + label, align_bytes=64),
+                )
+            words, scales = codes[key]
+            nc.vector.quantize_mx(
+                out=words[:, lo:hi].bitcast(dtype),
+                scales=scales[:, lo:hi],
+                in_=src[:, base + PACK * lo : base + PACK * hi],
+            )
+
+        def transposes(views):
+            bank = psum.tile([P, 4, P], F32, name="flipped", bufs=2)
+            for i in range(4):
+                nc.tensor.transpose(bank[:, i, :], views[i], ident[:])
+            return bank
+
+        def multiply(out, left, m, right, start, stop):
+            cols = slice(P * m, P * m + P)
+            nc.tensor.matmul_mx(
+                out=out,
+                lhsT=codes[left][0][:, cols].bitcast(E5M2),
+                lhsT_scale=codes[left][1][:, cols],
+                rhs=codes[right][0][:].bitcast(E4M3),
+                rhs_scale=codes[right][1][:],
+                start=start,
+                stop=stop,
+            )
+
+        def flip_g(b, half, engine):
+            dst = group_tile(("g", b), "grouped_gv", 3)
+            words = raw["g", b][:].bitcast(F32)
+            bank = transposes([words[:, 2 * half + i // 2, i % 2 :: 2] for i in range(4)])
             copy_words(
-                eng,
-                out=g_gr[b][:].bitcast(F32)[:, CH * half : CH * half + CH].rearrange("k (j n u) -> k j n u", j=2, u=2),
-                in_=xt[:].rearrange("k (j u) n -> k j n u", u=2),
+                engine,
+                out=dst[:].bitcast(F32)[:, PASS * half : PASS * half + PASS].rearrange(
+                    "k (j n v) -> k j n v", j=2, v=2
+                ),
+                in_=bank[:].rearrange("k (j v) n -> k j n v", v=2),
             )
 
         def quant_g(b, half):
-            quantise(gq, b, "gq", g_gr[b], E5, 256 * half, 256 * half + 256)
+            quantise(("g", b), E5M2, grouped["g", b], 2 * P * half, 2 * P * half + 2 * P)
 
-        def prep_w2(c, s, eng="s"):
-            if s == 0:
-                w2_gr[c] = stream.tile([P, 4 * CH], BF16, name="grouped_in", bufs=3, align_bytes=64)
-            words = w2_raw[c][:].rearrange("p s e d -> p (s e d)").bitcast(F32)
-            xt = bank_of_transposes(
-                [words[:, 256 * (2 * s + i // 2) + i % 2 : 256 * (2 * s + i // 2) + 256 : 2] for i in range(4)]
-            )
+        def flip_w2(c, u, s, engine):
+            dst = group_tile(("v", c, u), "grouped_gv", 3)
+            words = raw["v", c][:].bitcast(F32)
+            bank = transposes([words[:, s, u, i // 2, i % 2 :: 2] for i in range(4)])
             copy_words(
-                eng,
-                out=w2_gr[c][:].bitcast(F32)[:, CH * s : CH * s + CH].rearrange("k (n i) -> k n i", i=4),
-                in_=xt[:].rearrange("k i n -> k n i"),
+                engine,
+                out=dst[:].bitcast(F32)[:, PASS * s : PASS * s + PASS].rearrange("k (n i) -> k n i", i=4),
+                in_=bank[:].rearrange("k i n -> k n i"),
             )
 
-        def quant_w2(c, s=None):
-            if s is None:
-                quantise(w2q, c, "w2q", w2_gr[c], E4)
-            else:
-                quantise(w2q, c, "w2q", w2_gr[c], E4, 256 * s, 256 * s + 256)
+        def quant_w2(c, u):
+            quantise(("v", c, u), E4M3, grouped["v", c, u], 0, PASS)
 
-        def interleave(eng, dst, src, lo, hi):
-            o = dst[:, 4 * lo : 4 * hi].rearrange("p (c i t) -> p c t i", i=4, t=4)
-            i = src[:, :, lo:hi].rearrange("p t (c i) -> p c t i", i=4)
-            if eng == "s":
-                nc.scalar.copy(out=o, in_=i)
-            elif eng == "v":
-                nc.vector.tensor_copy(out=o, in_=i)
-            else:
-                nc.gpsimd.tensor_scalar(out=o, in0=i, scalar1=1.0, scalar2=0.0, op0=ALU.mult, op1=ALU.add)
-
-        def inter_raw(store, raw, i, eng, lo=0, hi=512):
-            if lo == 0:
-                store[i] = stream.tile([P, 4 * CH], BF16, name="grouped_raw", bufs=3, align_bytes=64)
-            interleave(eng, store[i], raw[i], lo, hi)
-
-        d_t, i_t, g_t = {}, {}, {}
-        dh_t = {}
-
-        def dh(k, j):
-            b, c = UNITS[k]
-            t = psum.tile([P, CH], F32, name="dh", bufs=3)
-            nc.tensor.matmul_mx(
-                out=t[:],
-                lhsT=gq[b][0][:, P * j : P * j + P].bitcast(E5),
-                lhsT_scale=gq[b][1][:, P * j : P * j + P],
-                rhs=w2q[c][0][:].bitcast(E4),
-                rhs_scale=w2q[c][1][:],
-                start=True,
-                stop=True,
+        def group_xw(what, i, half, engine):
+            dst = group_tile((what, i), "grouped_xw", 2)
+            cols = slice(2 * P * half, 2 * P * half + 2 * P)
+            interleave(
+                engine,
+                out=dst[:, PACK * cols.start : PACK * cols.stop],
+                in_=raw[what, i][:, :, cols].rearrange("p t (c i) -> p c t i", i=4),
             )
-            dh_t[k, j] = t
 
-        def dz(k, j):
-            if j == 0:
-                d_t[k] = stream.tile([P, 4, CH], BF16, name="dz", bufs=3, align_bytes=64)
+        def make_dh(b, c, u, j):
+            bank = psum.tile([P, PASS], F32, name="dh", bufs=3)
+            multiply(bank[:], ("g", b), j, ("v", c, u), True, True)
+            banks["dh", b, c, u, j] = bank
+
+        def make_dz(b, c, u, j):
+            if (b, c, u) not in dz:
+                dz[b, c, u] = stream.tile([P, 4, PASS], BF16, name="dz", bufs=4, align_bytes=64)
+            rows = pre_rows[b, c, j // 2][:, j % 2, :].rearrange("p (n u e) -> p n u e", u=2, e=2)
             nc.vector.scalar_tensor_tensor(
-                out=d_t[k][:, j, :], in0=pre_t[k][:, j, :], scalar=0.0, in1=dh_t[k, j][:], op0=ALU.max, op1=ALU.mult
+                out=dz[b, c, u][:, j, :].rearrange("p (n e) -> p n e", e=2),
+                in0=rows[:, :, u, :],
+                scalar=0.0,
+                in1=banks["dh", b, c, u, j][:].rearrange("p (n e) -> p n e", e=2),
+                op0=MAX,
+                op1=MULT,
             )
 
-        def flip(k, j0, n=2, eng="s"):
-            if j0 == 0:
-                g_t[k] = stream.tile([P, 4 * CH], BF16, name="dz_h", bufs=3, align_bytes=64)
-            words = d_t[k][:].bitcast(F32)
-            xt = psum.tile([P, 4, P], F32, name="xt", bufs=2)
-            for i in range(2 * n):
-                nc.tensor.transpose(xt[:, i, :], words[:, j0 + i // 2, i % 2 : 256 : 2], ident[:])
+        def flip_dz(b, c, j, engine):
+            dst = group_tile(("h", b, c), "grouped_h", 2, passes=2)
+            words = [dz[b, c, u][:, j, :].bitcast(F32) for u in range(2)]
+            bank = transposes([words[i % 2][:, P * (i // 2) : P * (i // 2) + P] for i in range(4)])
             copy_words(
-                eng,
-                out=g_t[k][:].bitcast(F32)[:, 256 * j0 : 256 * (j0 + n)].rearrange("k (j n u) -> k j n u", j=n, u=2),
-                in_=xt[:, 0 : 2 * n, :].rearrange("k (j u) n -> k j n u", u=2),
+                engine,
+                out=dst[:].bitcast(F32).rearrange("k (s n u) -> k s n u", s=2, u=2)[:, :, P * j : P * j + P, :],
+                in_=bank[:].rearrange("k (s u) n -> k s n u", u=2),
             )
 
-        def quant_h(k, j0=0, n=4):
-            quantise(hq, UNITS[k], "hq", g_t[k], E5, P * j0, P * (j0 + n))
+        def quant_h(b, c, s, j, n):
+            quantise(("h", b, 2 * c + s), E5M2, grouped["h", b, c], P * j, P * (j + n), PACK * PASS * s)
 
-        def quant_t(k, lo=0, hi=CH):
-            quantise(tq, UNITS[k], "tq", i_t[k], E5, lo, hi)
+        def group_t(b, c, u, e, s, engine):
+            dst = group_tile(("t", b, c, u), "grouped_t", 3)
+            first, n = (2 * P * e, 2 * P) if s == 2 else (2 * P * e + P * s, P)
+            src = dz[b, c, u][:].rearrange("p t (c i e) -> p e c t i", i=4, e=2)[:, e, :, :, :]
+            runs = slice(0, 2 * P // 4) if s == 2 else slice(P // 4 * s, P // 4 * (s + 1))
+            interleave(engine, out=dst[:, PACK * first : PACK * (first + n)], in_=src[:, runs, :, :])
 
-        def inter_dz(k, shares):
-            i_t[k] = stream.tile([P, 4 * CH], BF16, name="dz_t", bufs=3, align_bytes=64)
-            for eng, lo, hi in shares:
-                interleave(eng, i_t[k], d_t[k], lo, hi)
+        def quant_t(b, c, u, e):
+            lo, hi = (0, PASS) if e == 2 else (2 * P * e, 2 * P * e + 2 * P)
+            quantise(("t", b, 2 * c + u), E5M2, grouped["t", b, c, u], lo, hi)
 
-        def bank(tag):
-            if tag == "xt":
-                t = psum.tile([P, 4, P], F32, name="xt", bufs=2)
-                return t[:].rearrange("p a b -> p (a b)")
-            if tag == "dh":
-                t = psum.tile([P, CH], F32, name="dh", bufs=3)
-                return t[:]
-            t = psum.tile([P, DIM], F32, name="acc", bufs=3)
-            return t[:]
+        def add_pass(kind, a, m, q):
+            if q == 0:
+                tag, bufs = OTHER_BANKS.get((kind, a, m), ("out", 3))
+                banks[kind, a, m] = psum.tile([P, 4, P], F32, name=tag, bufs=bufs)[:].rearrange("p a b -> p (a b)")
+            left, right, last = (("h", a, q), ("w1", q), 3) if kind == "dx" else (("t", q, a), ("x", q), 1)
+            multiply(banks[kind, a, m], left, m, right, q == 0, q == last)
 
-        def leave(acc, dst, eng):
-            res = stream.tile([P, DIM], F32, name="res", bufs=8)
-            if eng == "s":
-                nc.scalar.activation(out=res[:], in_=acc, func=ACTF.Copy, scale=2.0)
+        def leave(kind, a, m, engine):
+            out = stream.tile([P, DIM], F32, name="out_rows", bufs=8)
+            if engine == "s":
+                nc.scalar.activation(out=out[:], in_=banks[kind, a, m], func=COPY, scale=2.0)
             else:
-                nc.vector.tensor_scalar(out=res[:], in0=acc, scalar1=2.0, scalar2=None, op0=ALU.mult)
-            nc.sync.dma_start(out=dst, in_=res[:])
-
-        def dst_of(kind, a, i):
+                nc.vector.tensor_scalar(out=out[:], in0=banks[kind, a, m], scalar1=2.0, scalar2=None, op0=MULT)
             if kind == "dx":
-                return out_0[a].rearrange("(p j) d -> p j d", j=4)[:, i, :]
-            return out_1[CH * a + P * i : CH * a + P * i + P, :]
-
-        opened = {}
-
-        def begin(kind, a, i, tag="acc"):
-            acc = bank(tag)
-            n = NC if kind == "dx" else B
-            for q in range(n - 1):
-                one_pass(acc, kind, a, i, q, n)
-            opened[kind, a, i] = acc
-
-        def one_pass(acc, kind, a, i, q, n):
-            if kind == "dx":
-                lhs, rhs = hq[a, q], w1q[q]
+                dst = out_0[a].rearrange("(p j) d -> p j d", j=4)[:, m, :]
             else:
-                lhs, rhs = tq[q, a], xq[q]
-            nc.tensor.matmul_mx(
-                out=acc,
-                lhsT=lhs[0][:, P * i : P * i + P].bitcast(E5),
-                lhsT_scale=lhs[1][:, P * i : P * i + P],
-                rhs=rhs[0][:].bitcast(E4),
-                rhs_scale=rhs[1][:],
-                start=(q == 0),
-                stop=(q == n - 1),
-            )
+                c, u, e, s = a // 2, a % 2, m // 2, m % 2
+                first = HALF * c + PASS * s
+                dst = out_1[first : first + PASS, :].rearrange("(p f) d -> p f d", f=4)[:, 2 * u + e, :]
+            nc.sync.dma_start(out=dst, in_=out[:])
 
-        def finish(kind, a, i, eng):
-            acc = opened[kind, a, i]
-            n = NC if kind == "dx" else B
-            one_pass(acc, kind, a, i, n - 1, n)
-            leave(acc, dst_of(kind, a, i), eng)
-
-        def whole(kind, a, i, eng="s", tag="acc"):
-            begin(kind, a, i, tag)
-            finish(kind, a, i, eng)
-
-        load_w2(0, 2)
-        load_g(0)
-        load_pre(0, 2)
-        load_w2(1)
-        load_pre(1, 2)
-        load_g(1)
-        load_pre(2)
-        load_x(0)
-        load_x(1)
-        load_pre(3)
-        load_w2(2)
-        load_w1(0)
-        load_pre(4)
-        load_w2(3)
-        load_w1(1)
-        load_pre(5)
-        load_w1(2)
-        load_w1(3)
-        load_pre(6)
-        load_pre(7)
-        pending = []
-
-        def emit(n, engs="s"):
-            for i in range(min(n, len(pending))):
-                kind, a, b = pending[0]
-                pending.remove(pending[0])
-                whole(kind, a, b, engs[i % len(engs)])
-
-        prep_w2(0, 0, "s")
-        prep_w2(0, 1, "v")
-        prep_g(0, 0, "s")
-        quant_w2(0)
-        prep_g(0, 1, "s")
-        quant_g(0, 0)
-        dh(0, 0)
-        dh(0, 1)
-        quant_g(0, 1)
-        dh(0, 2)
-
-        XENG = "g"
-        SHARE = [("v", 0, 512)]
-        LAST = [("v", 0, 256), ("s", 256, 512)]
-        for k in range(8):
-            nxt, last = k < 7, k == 7
-            dz(k, 0)
-            dh(k, 3)
-            if last:
-                flip(k, 0, 1)
-            emit(1)
-            if k >= 2:
-                inter_dz(k - 1, SHARE)
-            dz(k, 1)
-            if nxt:
-                flip(k, 0)
-            else:
-                flip(k, 1, 1)
-            if k >= 2:
-                quant_h(k - 1)
-            if k == 1:
-                quant_g(1, 0)
-                quant_g(1, 1)
-            if k == 3:
-                quant_w2(2)
-            if k == 4:
-                quant_w2(3)
-            if nxt and k >= 1:
-                dh(k + 1, 0)
-            emit(1)
-            dz(k, 2)
-            if nxt and k >= 1:
-                dh(k + 1, 1)
-            if last:
-                flip(k, 2, 1)
-            emit(1)
-            if k >= 2:
-                quant_t(k - 1)
-                if k == 3:
-                    pending.extend([("dw", 0, m) for m in range(4)])
-                if k == 4:
-                    pending.extend([("dw", 1, m) for m in range(4)])
-                if k == 6:
-                    pending.extend([("dx", 0, m) for m in range(4)])
-                if k == 7:
-                    pending.extend([("dw", 2, m) for m in range(4)])
-            if last:
-                quant_h(7, 0, 2)
-                emit(4)
-                begin("dx", 1, 0, "dh")
-            dz(k, 3)
-            flip(k, 2) if nxt else flip(k, 3, 1)
-            if nxt and k >= 1:
-                dh(k + 1, 2)
-            if k == 0:
-                inter_dz(0, SHARE)
-                prep_w2(1, 0)
-                prep_w2(1, 1)
-                quant_h(0)
-                quant_w2(1)
-                for j in range(3):
-                    dh(1, j)
-                quant_t(0)
-                prep_g(1, 0)
-                prep_g(1, 1)
-            if k == 2:
-                prep_w2(2, 0)
-                prep_w2(2, 1)
-            if k == 3:
-                prep_w2(3, 0)
-                prep_w2(3, 1)
-            if 2 <= k <= 5:
-                inter_raw(w1_gr, w1_raw, k - 2, "s", 0, 256)
-                inter_raw(w1_gr, w1_raw, k - 2, "s", 256, 512)
-            if k == 1:
-                inter_raw(x_gr, x_raw, 0, "v")
-                inter_raw(x_gr, x_raw, 1, XENG)
-            if k == 2:
-                quantise(xq, 0, "xq", x_gr[0], E4)
-                quantise(xq, 1, "xq", x_gr[1], E4)
-            if 3 <= k <= 6:
-                quantise(w1q, k - 3, "w1q", w1_gr[k - 3], E4)
-            emit(1)
-        begin("dx", 1, 1, "dh")
-        begin("dx", 1, 2)
-        begin("dx", 1, 3)
-        inter_dz(7, LAST)
-        finish("dx", 1, 0, "s")
-        finish("dx", 1, 1, "s")
-        quant_h(7, 2, 2)
-        begin("dw", 3, 0, "dh")
-        begin("dw", 3, 1)
-        begin("dw", 3, 2, "xt")
-        begin("dw", 3, 3, "xt")
-        quant_t(7, 0, 256)
-        finish("dx", 1, 2, "v")
-        finish("dx", 1, 3, "s")
-        finish("dw", 3, 0, "v")
-        quant_t(7, 256, 512)
-        finish("dw", 3, 1, "s")
-        finish("dw", 3, 2, "v")
-        finish("dw", 3, 3, "s")
+        steps = {
+            "load_g": load_g,
+            "load_x": load_x,
+            "load_w1": load_w1,
+            "load_w2": load_w2,
+            "load_pre": load_pre,
+            "flip_g": flip_g,
+            "quant_g": quant_g,
+            "flip_w2": flip_w2,
+            "quant_w2": quant_w2,
+            "group_x": lambda b, half, engine: group_xw("x", b, half, engine),
+            "quant_x": lambda b: quantise(("x", b), E4M3, grouped["x", b], 0, PASS),
+            "group_w1": lambda q, half, engine: group_xw("w1", q, half, engine),
+            "quant_w1": lambda q: quantise(("w1", q), E4M3, grouped["w1", q], 0, PASS),
+            "dh": make_dh,
+            "dz": make_dz,
+            "flip": flip_dz,
+            "quant_h": quant_h,
+            "group_t": group_t,
+            "quant_t": quant_t,
+            "dx_pass": lambda b, j, q: add_pass("dx", b, j, q),
+            "dx_out": lambda b, j, engine: leave("dx", b, j, engine),
+            "dw_pass": lambda cu, m, b: add_pass("dw", cu, m, b),
+            "dw_out": lambda cu, m, engine: leave("dw", cu, m, engine),
+        }
+        for row in SCHEDULE:
+            for word in row.split():
+                name, arguments = word.split(".")
+                steps[name](*[a if a in "svg" else int(a) for a in arguments])

from contextlib import ExitStack

import concourse.mybir as mybir
from concourse.masks import make_identity

BATCH, SEQ, DIM, HIDDEN = 2, 512, 512, 2048
P = 128
PACK = 4
PASS = P * PACK
HALF = HIDDEN // 2
FLOPS = 3 * 2 * BATCH * SEQ * DIM * HIDDEN

F32 = mybir.dt.float32
BF16 = mybir.dt.bfloat16
U32 = mybir.dt.uint32
U8 = mybir.dt.uint8
E4M3 = mybir.dt.float8_e4m3fn_x4
E5M2 = mybir.dt.float8_e5m2_x4
MULT, ADD, MAX = mybir.AluOpType.mult, mybir.AluOpType.add, mybir.AluOpType.max
COPY = mybir.ActivationFunctionType.Copy

SCHEDULE = (
    "load_g.01 load_w2.01 load_g.00 load_w2.00 load_x.0 flip_g.01v flip_w2.010s flip_w2.011v flip_g.00s",
    "  load_g.10 group_x.00v quant_w2.01 quant_g.00 load_g.11 flip_w2.001v group_x.01s load_pre.0001",
    "  flip_w2.000s quant_g.01 quant_x.0 flip_g.11s dh.0010 load_pre.0011 quant_w2.00 load_x.1 dh.0001",
    "dz.0010",
    "dz.0001 group_x.11s dh.0000 flip_g.10s dh.0011 dh.0012 load_w2.12 load_pre.0021 group_x.10g",
    "dz.0000 flip.000s load_pre.0031",
    "dz.0011 quant_x.1 load_pre.1022 flip_w2.101s quant_g.11 dh.0002 load_pre.1002 dh.0003 flip_w2.100s",
    "  flip_w2.111s quant_g.10",
    "dz.0012 dh.0013",
    "dz.0002 load_pre.0102",
    "dz.0003 quant_w2.10 dh.1003 group_t.00002s flip.002s",
    "dz.0013 group_t.00012g flip_w2.110s dh.1013",
    "dz.1003 dh.1002 flip.001s",
    "dz.1013 group_t.00102s dh.1000",
    "dz.1002 dh.1001 flip.103s dh.1011 quant_t.0002",
    "dz.1001",
    "dz.1000 flip.003s group_t.00112g group_t.10012s load_w1.0 load_w1.1 dw_pass.020",
    "dz.1011 load_pre.0122 dh.1010 quant_w2.11 dh.1012 flip.101s group_t.10002g group_w1.00s dh.0101",
    "  group_w1.01s",
    "dz.1012",
    "dz.1010",
    "dz.0101 dh.0111 load_pre.1122 dw_pass.000 quant_t.0012 dh.0103 flip.100s quant_t.1002 load_w1.2",
    "  dw_pass.120 quant_h.00004 dw_pass.021 load_pre.1102 quant_h.00104 dw_out.02s",
    "dz.0111 dh.0113",
    "dz.0103 flip.102s dw_pass.001 load_w1.3 dh.0100",
    "dz.0113 dw_pass.030 group_t.10102g dw_pass.031",
    "dz.0100 group_w1.11g dh.0102 group_t.10112s",
    "dz.0102 quant_t.1012 dw_out.00s flip.011s group_w1.10s dh.1113 dh.0110 quant_w1.0",
    "dz.1113 flip.013s",
    "dz.0110 group_t.01012g dw_pass.100 dw_pass.010 dw_pass.121 dw_pass.011 dh.1102 group_t.01002g dh.1112",
    "  dw_pass.101 dh.1103 dw_out.12s",
    "dz.1112 dw_out.10s flip.010s",
    "dz.1102",
    "dz.1103 quant_h.10004 dw_pass.130 dh.0112 dh.1110 quant_h.10104 dw_out.01s dw_out.03s dh.1111",
    "  quant_w1.1 group_w1.20g",
    "dz.0112 dw_pass.131",
    "dz.1110 group_w1.21s flip.113s flip.112s dx_pass.030 dx_pass.031 dx_pass.110",
    "dz.1111 dx_pass.111 dh.1100",
    "dz.1100 dw_out.13s flip.012s dh.1101 group_w1.30s",
    "dz.1101 group_w1.31g quant_w1.2 quant_h.01004 quant_h.01104 quant_h.11022 dw_pass.110 dx_pass.130",
    "  dx_pass.000 dx_pass.001 quant_w1.3 dw_pass.111 flip.110s quant_h.11122 flip.111s quant_h.11002",
    "  dx_pass.120 dx_pass.121 dx_pass.100 dx_pass.002 dx_pass.020 dx_pass.032 dw_out.11s dx_pass.122",
    "  group_t.11012s dx_pass.003 dx_pass.033 dx_out.00v dx_pass.101 dx_pass.123 dx_pass.112 dx_pass.102",
    "  quant_h.11102 dx_pass.103 dx_out.03s group_t.11002v dx_pass.113 dx_out.12s dx_pass.131 dx_out.10s",
    "  dx_pass.132 dx_pass.133 quant_t.0102 quant_t.1102 dw_pass.200 dx_out.11s dw_pass.230 group_t.11100g",
    "  dx_out.13v dw_pass.201 dw_pass.231 dw_pass.220 dw_pass.210 dw_pass.221 dw_out.20v dw_out.23v",
    "  dx_pass.021 group_t.01112g dw_out.22v dx_pass.022 group_t.11111s dx_pass.023 dx_pass.010",
    "  group_t.11101s dw_pass.211 dx_pass.011 group_t.01102s dx_pass.012 group_t.11110v quant_t.0112",
    "  dx_pass.013 dw_pass.310 quant_t.1110 dw_pass.311 dx_out.02s quant_t.1111 dw_pass.330 dw_out.21s",
    "  dx_out.01s dw_pass.331 dw_pass.320 dw_pass.321 dw_pass.300 dw_out.31v dw_out.33v dw_out.32v",
    "  dw_pass.301 dw_out.30v",
)

OTHER_BANKS = {
    ("dw", 0, 1): ("flipped", 2),
    ("dw", 1, 1): ("dh", 3),
    ("dw", 2, 0): ("dh", 3),
    ("dw", 2, 2): ("dh", 3),
    ("dw", 2, 3): ("dh", 3),
    ("dw", 3, 0): ("dh", 3),
    ("dw", 3, 1): ("flipped", 2),
    ("dw", 3, 3): ("flipped", 2),
    ("dx", 0, 0): ("dh", 3),
    ("dx", 0, 2): ("flipped", 2),
    ("dx", 1, 0): ("flipped", 2),
    ("dx", 1, 2): ("dh", 3),
}


def tile_mlp_v_kernel(tc, x, w1, w2, pre, grad_out, out_0, out_1):
    nc = tc.nc
    with ExitStack() as ctx:
        keep = ctx.enter_context(tc.tile_pool(name="keep", bufs=1))
        stream = ctx.enter_context(tc.tile_pool(name="stream", bufs=2))
        psum = ctx.enter_context(tc.psum_pool(name="psum", bufs=2))
        ctx.enter_context(tc.manual_schedule())

        ident = keep.tile([P, P], F32, name="ident")
        make_identity(nc, ident[:])
        warm = keep.tile([P, 1], F32, name="warm")
        nc.vector.memset(warm[:], 0.0)
        nc.scalar.activation(out=warm[:], in_=warm[:], func=COPY, scale=2.0)

        raw = {}
        pre_rows = {}
        grouped = {}
        dz = {}
        banks = {}
        codes = {}

        def load_g(b, half):
            if ("g", b) not in raw:
                raw["g", b] = keep.tile([P, 4, DIM], BF16, name="g_raw%d" % b)
            j = slice(2 * half, 2 * half + 2)
            src = grad_out[b].rearrange("(p j) d -> p j d", j=4)
            nc.sync.dma_start(out=raw["g", b][:, j, :], in_=src[:, j, :])

        def load_x(b):
            raw["x", b] = stream.tile([P, 4, DIM], BF16, name="xw_raw", bufs=4)
            nc.sync.dma_start(out=raw["x", b][:], in_=x[b].rearrange("(p j) d -> p j d", j=4))

        def load_w1(q):
            raw["w1", q] = stream.tile([P, 4, DIM], BF16, name="xw_raw", bufs=4)
            src = w1[PASS * q : PASS * q + PASS, :].rearrange("(p t) d -> p t d", t=4)
            nc.sync.dma_start(out=raw["w1", q][:], in_=src)

        def load_w2(c, u):
            if ("v", c) not in raw:
                raw["v", c] = stream.tile([P, 2, 2, 2, DIM], BF16, name="w2_raw", bufs=2)
            rows = w2[HALF * c : HALF * c + HALF, :]
            if u == 2:
                nc.sync.dma_start(
                    out=raw["v", c][:].rearrange("p s u e d -> p s (u e d)"),
                    in_=rows.rearrange("(s p f) d -> p s (f d)", s=2, f=4),
                )
            else:
                nc.sync.dma_start(
                    out=raw["v", c][:].rearrange("p s u e d -> p s u (e d)")[:, :, u, :],
                    in_=rows.rearrange("(s p u e) d -> p s u (e d)", s=2, u=2, e=2)[:, :, u, :],
                )

        def load_pre(b, c, j, n):
            if (b, c, j // 2) not in pre_rows:
                pre_rows[b, c, j // 2] = stream.tile([P, 2, HALF], F32, name="pre_rows", bufs=5)
            src = pre[b].rearrange("(p j) h -> p j h", j=4)
            nc.sync.dma_start(
                out=pre_rows[b, c, j // 2][:, j % 2 : j % 2 + n, :],
                in_=src[:, j : j + n, HALF * c : HALF * c + HALF],
            )

        def copy_words(engine, out, in_):
            if engine == "s":
                nc.scalar.copy(out=out, in_=in_)
            else:
                nc.vector.tensor_copy(out=out, in_=in_)

        def interleave(engine, out, in_):
            out = out.rearrange("p (c i t) -> p c t i", i=4, t=4)
            if engine == "s":
                nc.scalar.copy(out=out, in_=in_)
            elif engine == "v":
                nc.vector.tensor_copy(out=out, in_=in_)
            else:
                nc.gpsimd.tensor_scalar(out=out, in0=in_, scalar1=1.0, scalar2=0.0, op0=MULT, op1=ADD)

        def group_tile(key, name, bufs, passes=1):
            if key not in grouped:
                grouped[key] = stream.tile([P, passes * PACK * PASS], BF16, name=name, bufs=bufs, align_bytes=64)
            return grouped[key]

        def quantise(key, dtype, src, lo, hi, base=0):
            if key not in codes:
                label = "_".join([str(k) for k in key])
                codes[key] = (
                    keep.tile([P, PASS], U32, name="codes_" + label, align_bytes=64),
                    keep.tile([P, PASS], U8, name="scales_" + label, align_bytes=64),
                )
            words, scales = codes[key]
            nc.vector.quantize_mx(
                out=words[:, lo:hi].bitcast(dtype),
                scales=scales[:, lo:hi],
                in_=src[:, base + PACK * lo : base + PACK * hi],
            )

        def transposes(views):
            bank = psum.tile([P, 4, P], F32, name="flipped", bufs=2)
            for i in range(4):
                nc.tensor.transpose(bank[:, i, :], views[i], ident[:])
            return bank

        def multiply(out, left, m, right, start, stop):
            cols = slice(P * m, P * m + P)
            nc.tensor.matmul_mx(
                out=out,
                lhsT=codes[left][0][:, cols].bitcast(E5M2),
                lhsT_scale=codes[left][1][:, cols],
                rhs=codes[right][0][:].bitcast(E4M3),
                rhs_scale=codes[right][1][:],
                start=start,
                stop=stop,
            )

        def flip_g(b, half, engine):
            dst = group_tile(("g", b), "grouped_gv", 3)
            words = raw["g", b][:].bitcast(F32)
            bank = transposes([words[:, 2 * half + i // 2, i % 2 :: 2] for i in range(4)])
            copy_words(
                engine,
                out=dst[:].bitcast(F32)[:, PASS * half : PASS * half + PASS].rearrange(
                    "k (j n v) -> k j n v", j=2, v=2
                ),
                in_=bank[:].rearrange("k (j v) n -> k j n v", v=2),
            )

        def quant_g(b, half):
            quantise(("g", b), E5M2, grouped["g", b], 2 * P * half, 2 * P * half + 2 * P)

        def flip_w2(c, u, s, engine):
            dst = group_tile(("v", c, u), "grouped_gv", 3)
            words = raw["v", c][:].bitcast(F32)
            bank = transposes([words[:, s, u, i // 2, i % 2 :: 2] for i in range(4)])
            copy_words(
                engine,
                out=dst[:].bitcast(F32)[:, PASS * s : PASS * s + PASS].rearrange("k (n i) -> k n i", i=4),
                in_=bank[:].rearrange("k i n -> k n i"),
            )

        def quant_w2(c, u):
            quantise(("v", c, u), E4M3, grouped["v", c, u], 0, PASS)

        def group_xw(what, i, half, engine):
            dst = group_tile((what, i), "grouped_xw", 2)
            cols = slice(2 * P * half, 2 * P * half + 2 * P)
            interleave(
                engine,
                out=dst[:, PACK * cols.start : PACK * cols.stop],
                in_=raw[what, i][:, :, cols].rearrange("p t (c i) -> p c t i", i=4),
            )

        def make_dh(b, c, u, j):
            bank = psum.tile([P, PASS], F32, name="dh", bufs=3)
            multiply(bank[:], ("g", b), j, ("v", c, u), True, True)
            banks["dh", b, c, u, j] = bank

        def make_dz(b, c, u, j):
            if (b, c, u) not in dz:
                dz[b, c, u] = stream.tile([P, 4, PASS], BF16, name="dz", bufs=4, align_bytes=64)
            rows = pre_rows[b, c, j // 2][:, j % 2, :].rearrange("p (n u e) -> p n u e", u=2, e=2)
            nc.vector.scalar_tensor_tensor(
                out=dz[b, c, u][:, j, :].rearrange("p (n e) -> p n e", e=2),
                in0=rows[:, :, u, :],
                scalar=0.0,
                in1=banks["dh", b, c, u, j][:].rearrange("p (n e) -> p n e", e=2),
                op0=MAX,
                op1=MULT,
            )

        def flip_dz(b, c, j, engine):
            dst = group_tile(("h", b, c), "grouped_h", 2, passes=2)
            words = [dz[b, c, u][:, j, :].bitcast(F32) for u in range(2)]
            bank = transposes([words[i % 2][:, P * (i // 2) : P * (i // 2) + P] for i in range(4)])
            copy_words(
                engine,
                out=dst[:].bitcast(F32).rearrange("k (s n u) -> k s n u", s=2, u=2)[:, :, P * j : P * j + P, :],
                in_=bank[:].rearrange("k (s u) n -> k s n u", u=2),
            )

        def quant_h(b, c, s, j, n):
            quantise(("h", b, 2 * c + s), E5M2, grouped["h", b, c], P * j, P * (j + n), PACK * PASS * s)

        def group_t(b, c, u, e, s, engine):
            dst = group_tile(("t", b, c, u), "grouped_t", 3)
            first, n = (2 * P * e, 2 * P) if s == 2 else (2 * P * e + P * s, P)
            src = dz[b, c, u][:].rearrange("p t (c i e) -> p e c t i", i=4, e=2)[:, e, :, :, :]
            runs = slice(0, 2 * P // 4) if s == 2 else slice(P // 4 * s, P // 4 * (s + 1))
            interleave(engine, out=dst[:, PACK * first : PACK * (first + n)], in_=src[:, runs, :, :])

        def quant_t(b, c, u, e):
            lo, hi = (0, PASS) if e == 2 else (2 * P * e, 2 * P * e + 2 * P)
            quantise(("t", b, 2 * c + u), E5M2, grouped["t", b, c, u], lo, hi)

        def add_pass(kind, a, m, q):
            if q == 0:
                tag, bufs = OTHER_BANKS.get((kind, a, m), ("out", 3))
                banks[kind, a, m] = psum.tile([P, 4, P], F32, name=tag, bufs=bufs)[:].rearrange("p a b -> p (a b)")
            left, right, last = (("h", a, q), ("w1", q), 3) if kind == "dx" else (("t", q, a), ("x", q), 1)
            multiply(banks[kind, a, m], left, m, right, q == 0, q == last)

        def leave(kind, a, m, engine):
            out = stream.tile([P, DIM], F32, name="out_rows", bufs=8)
            if engine == "s":
                nc.scalar.activation(out=out[:], in_=banks[kind, a, m], func=COPY, scale=2.0)
            else:
                nc.vector.tensor_scalar(out=out[:], in0=banks[kind, a, m], scalar1=2.0, scalar2=None, op0=MULT)
            if kind == "dx":
                dst = out_0[a].rearrange("(p j) d -> p j d", j=4)[:, m, :]
            else:
                c, u, e, s = a // 2, a % 2, m // 2, m % 2
                first = HALF * c + PASS * s
                dst = out_1[first : first + PASS, :].rearrange("(p f) d -> p f d", f=4)[:, 2 * u + e, :]
            nc.sync.dma_start(out=dst, in_=out[:])

        steps = {
            "load_g": load_g,
            "load_x": load_x,
            "load_w1": load_w1,
            "load_w2": load_w2,
            "load_pre": load_pre,
            "flip_g": flip_g,
            "quant_g": quant_g,
            "flip_w2": flip_w2,
            "quant_w2": quant_w2,
            "group_x": lambda b, half, engine: group_xw("x", b, half, engine),
            "quant_x": lambda b: quantise(("x", b), E4M3, grouped["x", b], 0, PASS),
            "group_w1": lambda q, half, engine: group_xw("w1", q, half, engine),
            "quant_w1": lambda q: quantise(("w1", q), E4M3, grouped["w1", q], 0, PASS),
            "dh": make_dh,
            "dz": make_dz,
            "flip": flip_dz,
            "quant_h": quant_h,
            "group_t": group_t,
            "quant_t": quant_t,
            "dx_pass": lambda b, j, q: add_pass("dx", b, j, q),
            "dx_out": lambda b, j, engine: leave("dx", b, j, engine),
            "dw_pass": lambda cu, m, b: add_pass("dw", cu, m, b),
            "dw_out": lambda cu, m, engine: leave("dw", cu, m, engine),
        }
        for row in SCHEDULE:
            for word in row.split():
                name, arguments = word.split(".")
                steps[name](*[a if a in "svg" else int(a) for a in arguments])
